import numpy as np
import ml_dtypes


def mxq(x, axis, fmt="e4m3"):
    dtype, down = {"e4m3": (ml_dtypes.float8_e4m3fn, 7), "e5m2": (ml_dtypes.float8_e5m2, 14)}[fmt]
    v = np.moveaxis(np.asarray(x, np.float32).astype(ml_dtypes.bfloat16).astype(np.float64), axis, -1)
    blocks = v.reshape(v.shape[:-1] + (-1, 32))
    amax = np.abs(blocks).max(-1, keepdims=True)
    byte = np.maximum(np.where(amax > 0, np.frexp(amax)[1] - 1 + 127, 0) - down, 1)
    scale = np.exp2(byte - 127.0)
    codes = (blocks / scale).astype(np.float32).astype(dtype).astype(np.float64)
    return np.moveaxis((codes * scale).reshape(v.shape), -1, axis)


WIDE = False


def mx_kscale(k):
    if not WIDE:
        return np.ones(k)
    levels = np.array([10, -10, 5, -5, 0])
    if k % 512:
        return np.exp2(np.random.permutation(np.resize(levels, k // 32))).repeat(32)
    a = np.empty((k // 512, 16))
    for p in range(k // 512):
        a[p, :8] = np.random.permutation(np.resize(levels, 8))
        for g in range(8):
            far = levels[np.abs(levels - a[p, g]) >= 10]
            a[p, g + 8] = far[np.random.randint(len(far))]
    return np.exp2(a.ravel()).repeat(32)


BF16 = ml_dtypes.bfloat16


def bf(x):
    return np.asarray(x, np.float32).astype(BF16)


def f64(x):
    return np.asarray(x).astype(np.float64)


B, C, MID, HH, WW = 1, 2048, 512, 32, 32
N = HH * WW


def setup_inputs():
    s, t = mx_kscale(N), mx_kscale(MID)
    a = np.exp(1.5 * np.random.standard_normal((B, N, N)))
    a = a / a.sum(-1, keepdims=True)
    return {
        "attn": bf(a * s),
        "h_x": bf(np.random.standard_normal((B, MID, N)) * 2.0 * t[:, None] / s),
        "v_w": bf(np.random.standard_normal((C, MID)) * 3.0 / np.sqrt(MID) / t),
        "v_b": bf(np.random.standard_normal(C) * 0.3),
        "x": bf(np.random.standard_normal((B, C, HH, WW))),
    }


def reference(attn, h_x, v_w, v_b, x):
    z = mxq(f64(h_x), 2, "e4m3") @ mxq(f64(attn), 2, "e4m3").transpose(0, 2, 1)
    y = (mxq(f64(v_w), 1, "e4m3") @ mxq(z, 1, "e4m3")) + f64(v_b)[None, :, None]
    return y.reshape(B, C, HH, WW) + f64(x)

@@ -1,0 +1,226 @@
+from contextlib import ExitStack
+
+import concourse.mybir as mybir
+from concourse.masks import make_identity
+
+F32 = mybir.dt.float32
+BF16 = mybir.dt.bfloat16
+U32 = mybir.dt.uint32
+U8 = mybir.dt.uint8
+FP8X4 = mybir.dt.float8_e4m3fn_x4
+ADD = mybir.AluOpType.add
+IDENTITY = mybir.ActivationFunctionType.Identity
+
+P = 128
+PACK = 4
+K_PASS = P * PACK
+POS = 1024
+MID = 512
+OUT_CH = 2048
+HALF = POS // 2
+PASSES_M = POS // K_PASS
+JOB = 512
+BANK_COLS = JOB // 2
+QUAD = 4
+QUADS = OUT_CH // (QUAD * P)
+PSUM_BANKS = 8
+STEPS = 4
+TURN_AFTER = 0
+QUANTISE_AFTER = 1
+
+FLOPS = 2 * MID * POS * POS + 2 * OUT_CH * MID * POS
+
+
+def mx_tiles(pool, name):
+    return {
+        "grouped": pool.tile([P, JOB * PACK], BF16, name=name + "_grouped", align_bytes=64),
+        "codes": pool.tile([P, JOB], U32, name=name + "_codes", align_bytes=64),
+        "scales": pool.tile([P, JOB], U8, name=name + "_scales", align_bytes=64),
+    }
+
+
+def quantise(nc, operand, first_col, cols):
+    nc.vector.quantize_mx(
+        out=operand["codes"][:, first_col : first_col + cols].bitcast(FP8X4),
+        scales=operand["scales"][:, first_col : first_col + cols],
+        in_=operand["grouped"][:, first_col * PACK : (first_col + cols) * PACK],
+    )
+
+
+def turn_bank(nc, psum, identity, row_tiles, first_word, operand, bank_index):
+    turned = psum.tile([P, 2, BANK_COLS], F32, tag="bank")
+    for u in range(2):
+        for r in range(2):
+            nc.tensor.transpose(
+                turned[:, u, r * P : (r + 1) * P],
+                row_tiles[r][:, first_word + u : first_word + 2 * P : 2],
+                identity[:],
+            )
+    grouped_words = operand["grouped"][:].bitcast(F32).rearrange(
+        "p (b c u) -> p b c u", b=2, u=2
+    )
+    nc.scalar.copy(out=grouped_words[:, bank_index], in_=turned[:].rearrange("p u c -> p c u"))
+
+
+def tile_soablock_pb_kernel(tc, attn, h_x, v_w, v_b, x, out):
+    nc = tc.nc
+    with ExitStack() as ctx:
+        ctx.enter_context(tc.manual_schedule())
+        keep = ctx.enter_context(tc.tile_pool(name="keep", bufs=1))
+        psum = ctx.enter_context(tc.psum_pool(name="psum", bufs=PSUM_BANKS))
+
+        x_rows = x[0].rearrange("(p i) hh ww -> p i (hh ww)", i=QUAD * QUADS)
+        out_rows = out[0].rearrange("(p i) hh ww -> p i (hh ww)", i=QUAD * QUADS)
+        vw_rows = v_w.rearrange("(p i) c -> p i c", i=QUAD * QUADS)
+
+        hx_raw = [keep.tile([P, 2, POS], BF16, name="hx_raw%d" % u) for u in range(2)]
+        at_raw = [keep.tile([P, 2, POS], BF16, name="at_raw%d" % q) for q in range(4)]
+        vw_raw = [keep.tile([P, QUAD, MID], BF16, name="vw_raw%d" % k) for k in range(QUADS)]
+        x_sb = [keep.tile([P, QUAD, POS], BF16, name="x_sb%d" % k) for k in range(QUADS)]
+
+        def load_attention(q):
+            half_rows = attn[0, (q // 2) * HALF : (q // 2 + 1) * HALF, :]
+            first_j = 2 * (q % 2)
+            nc.sync.dma_start(
+                out=at_raw[q][:],
+                in_=half_rows.rearrange("(p j) m -> p j m", j=4)[:, first_j : first_j + 2, :],
+            )
+
+        def load_weights(k):
+            nc.sync.dma_start(out=vw_raw[k][:], in_=vw_rows[:, k * QUAD : (k + 1) * QUAD, :])
+
+        def load_residual(k):
+            nc.sync.dma_start(out=x_sb[k][:], in_=x_rows[:, k * QUAD : (k + 1) * QUAD, :])
+
+        for u in range(2):
+            nc.sync.dma_start(
+                out=hx_raw[u][:],
+                in_=h_x[0].rearrange("(p t) m -> p t m", t=PACK)[:, 2 * u : 2 * (u + 1), :],
+            )
+        for q in range(4):
+            load_attention(q)
+        for k in range(QUADS):
+            load_weights(k)
+            load_residual(k)
+
+        bias_bf16 = keep.tile([P, QUAD * QUADS], BF16)
+        nc.scalar.dma_start(out=bias_bf16[:], in_=v_b.rearrange("(p i) -> p i", i=QUAD * QUADS))
+        bias = keep.tile([P, QUAD * QUADS], F32)
+        nc.scalar.activation(out=bias[:], in_=bias_bf16[:], func=IDENTITY)
+
+        identity = keep.tile([P, P], F32)
+        make_identity(nc, identity[:])
+
+        hx_mx = [mx_tiles(keep, "hx%d" % u) for u in range(2)]
+        at_mx = [mx_tiles(keep, "at%d" % q) for q in range(4)]
+        vw_mx = [mx_tiles(keep, "vw%d" % k) for k in range(QUADS)]
+        z_mx = [mx_tiles(keep, "z%d" % h) for h in range(2)]
+
+        def prepare_values(u):
+            words = hx_raw[u][:].bitcast(F32)
+            for g in range(PASSES_M):
+                turn_bank(nc, psum, identity, [words[:, e, :] for e in range(2)],
+                          g * 2 * P, hx_mx[u], g)
+            quantise(nc, hx_mx[u], 0, JOB)
+
+        def prepare_attention(q):
+            words = at_raw[q][:].bitcast(F32)
+            rows = [words[:, s, :] for s in range(2)]
+            for g in range(PASSES_M):
+                turn_bank(nc, psum, identity, rows, g * 2 * P, at_mx[q], g)
+            quantise(nc, at_mx[q], 0, JOB)
+
+        def turn_weights(k):
+            words = vw_raw[k][:].bitcast(F32)
+            for b in range(2):
+                turn_bank(nc, psum, identity, [words[:, 2 * b + r, :] for r in range(2)],
+                          0, vw_mx[k], b)
+
+        def mix_positions(q):
+            h = q // 2
+            grouped = z_mx[h]["grouped"][:].rearrange("p (j n t) -> p j n t", j=4, t=PACK)
+            for s in range(2):
+                z_bank = psum.tile([P, PACK, P], F32, tag="bank")
+                for t in range(PACK):
+                    for g in range(PASSES_M):
+                        lhs_cols = slice(g * 2 * P + (t % 2) * P, g * 2 * P + (t % 2 + 1) * P)
+                        rhs_cols = slice(g * 2 * P + s * P, g * 2 * P + (s + 1) * P)
+                        nc.tensor.matmul_mx(
+                            out=z_bank[:, t, :],
+                            lhsT=hx_mx[t // 2]["codes"][:, lhs_cols].bitcast(FP8X4),
+                            lhsT_scale=hx_mx[t // 2]["scales"][:, lhs_cols],
+                            rhs=at_mx[q]["codes"][:, rhs_cols].bitcast(FP8X4),
+                            rhs_scale=at_mx[q]["scales"][:, rhs_cols],
+                            start=(g == 0),
+                            stop=(g == PASSES_M - 1),
+                        )
+                copy = nc.vector.tensor_copy if s == 0 else nc.scalar.copy
+                copy(out=grouped[:, 2 * (q % 2) + s], in_=z_bank[:].rearrange("p t n -> p n t"))
+            quantise(nc, z_mx[h], (q % 2) * BANK_COLS, BANK_COLS)
+
+        out_sb = [keep.tile([P, 2, POS], F32, name="out_sb%d" % r) for r in range(2 * QUADS)]
+
+        def expand_channels(k, pair, h):
+            for r in range(2):
+                i = 2 * pair + r
+                y_bank = psum.tile([P, HALF], F32, tag="bank")
+                nc.tensor.matmul_mx(
+                    out=y_bank[:],
+                    lhsT=vw_mx[k]["codes"][:, i * P : (i + 1) * P].bitcast(FP8X4),
+                    lhsT_scale=vw_mx[k]["scales"][:, i * P : (i + 1) * P],
+                    rhs=z_mx[h]["codes"][:].bitcast(FP8X4),
+                    rhs_scale=z_mx[h]["scales"][:],
+                    start=True,
+                    stop=True,
+                )
+                positions = slice(h * HALF, (h + 1) * HALF)
+                y_in_order = y_bank[:].rearrange("p (j n) -> p n j", j=4)
+                result = out_sb[2 * k + pair][:, r, positions]
+                residual = x_sb[k][:, i, positions]
+                tile_bias = bias[:, k * QUAD + i : k * QUAD + i + 1]
+                if r == 0 and h == 0:
+                    nc.scalar.activation(
+                        out=result.rearrange("p (n j) -> p n j", j=4),
+                        in_=y_in_order,
+                        func=IDENTITY,
+                        bias=tile_bias,
+                    )
+                    nc.gpsimd.tensor_tensor(out=result, in0=result, in1=residual, op=ADD)
+                else:
+                    nc.vector.scalar_tensor_tensor(
+                        out=result.rearrange("p (n j) -> p n j", j=4),
+                        in0=y_in_order,
+                        scalar=tile_bias,
+                        in1=residual.rearrange("p (n j) -> p n j", j=4),
+                        op0=ADD,
+                        op1=ADD,
+                    )
+
+        def store_pair(k, pair):
+            first_row = k * QUAD + 2 * pair
+            nc.sync.dma_start(
+                out=out_rows[:, first_row : first_row + 2, :], in_=out_sb[2 * k + pair][:]
+            )
+
+        prepare_values(0)
+        prepare_values(1)
+        prepare_attention(0)
+        prepare_attention(1)
+        prepare_attention(2)
+        mix_positions(0)
+        prepare_attention(3)
+        turn_weights(0)
+        quantise(nc, vw_mx[0], 0, JOB)
+        mix_positions(1)
+        mix_positions(2)
+        mix_positions(3)
+        for k in range(QUADS):
+            for step in range(STEPS):
+                pair, h = divmod(step, 2)
+                expand_channels(k, pair, h)
+                if k + 1 < QUADS and step == TURN_AFTER:
+                    turn_weights(k + 1)
+                if k + 1 < QUADS and step == QUANTISE_AFTER:
+                    quantise(nc, vw_mx[k + 1], 0, JOB)
+                if h == 1:
+                    store_pair(k, pair)

@@ -74,34 +74,34 @@ def tile_soablock_pb_kernel(tc, attn, h_x, v_w, v_b, x, out):
         vw_rows = v_w.rearrange("(p i) c -> p i c", i=QUAD * QUADS)
 
         hx_raw = [keep.tile([P, 2, POS], BF16, name="hx_raw%d" % u) for u in range(2)]
-        at_raw = [keep.tile([P, 2, POS], BF16, name="at_raw%d" % q) for q in range(4)]
-        vw_raw = [keep.tile([P, QUAD, MID], BF16, name="vw_raw%d" % k) for k in range(QUADS)]
-        x_sb = [keep.tile([P, QUAD, POS], BF16, name="x_sb%d" % k) for k in range(QUADS)]
+        at_raw = [keep.tile([P, 4, POS], BF16, name="at_raw%d" % h) for h in range(2)]
+        vw_raw = [keep.tile([P, 2 * QUAD, MID], BF16, name="vw_raw%d" % d) for d in range(2)]
+        x_sb = [keep.tile([P, 2 * QUAD, POS], BF16, name="x_sb%d" % d) for d in range(2)]
 
-        def load_attention(q):
-            half_rows = attn[0, (q // 2) * HALF : (q // 2 + 1) * HALF, :]
-            first_j = 2 * (q % 2)
+        def load_attention(h):
+            half_rows = attn[0, h * HALF : (h + 1) * HALF, :]
             nc.sync.dma_start(
-                out=at_raw[q][:],
-                in_=half_rows.rearrange("(p j) m -> p j m", j=4)[:, first_j : first_j + 2, :],
+                out=at_raw[h][:], in_=half_rows.rearrange("(p j) m -> p j m", j=4)
             )
 
-        def load_weights(k):
-            nc.sync.dma_start(out=vw_raw[k][:], in_=vw_rows[:, k * QUAD : (k + 1) * QUAD, :])
+        def load_weights(d):
+            rows = slice(d * 2 * QUAD, (d + 1) * 2 * QUAD)
+            nc.sync.dma_start(out=vw_raw[d][:], in_=vw_rows[:, rows, :])
 
-        def load_residual(k):
-            nc.sync.dma_start(out=x_sb[k][:], in_=x_rows[:, k * QUAD : (k + 1) * QUAD, :])
+        def load_residual(d):
+            rows = slice(d * 2 * QUAD, (d + 1) * 2 * QUAD)
+            nc.sync.dma_start(out=x_sb[d][:], in_=x_rows[:, rows, :])
 
         for u in range(2):
             nc.sync.dma_start(
                 out=hx_raw[u][:],
                 in_=h_x[0].rearrange("(p t) m -> p t m", t=PACK)[:, 2 * u : 2 * (u + 1), :],
             )
-        for q in range(4):
-            load_attention(q)
-        for k in range(QUADS):
-            load_weights(k)
-            load_residual(k)
+        for h in range(2):
+            load_attention(h)
+        for d in range(2):
+            load_weights(d)
+            load_residual(d)
 
         bias_bf16 = keep.tile([P, QUAD * QUADS], BF16)
         nc.scalar.dma_start(out=bias_bf16[:], in_=v_b.rearrange("(p i) -> p i", i=QUAD * QUADS))
@@ -124,17 +124,18 @@ def tile_soablock_pb_kernel(tc, attn, h_x, v_w, v_b, x, out):
             quantise(nc, hx_mx[u], 0, JOB)
 
         def prepare_attention(q):
-            words = at_raw[q][:].bitcast(F32)
-            rows = [words[:, s, :] for s in range(2)]
+            words = at_raw[q // 2][:].bitcast(F32)
+            rows = [words[:, 2 * (q % 2) + s, :] for s in range(2)]
             for g in range(PASSES_M):
                 turn_bank(nc, psum, identity, rows, g * 2 * P, at_mx[q], g)
             quantise(nc, at_mx[q], 0, JOB)
 
         def turn_weights(k):
-            words = vw_raw[k][:].bitcast(F32)
+            words = vw_raw[k // 2][:].bitcast(F32)
+            first_tile = (k % 2) * QUAD
             for b in range(2):
-                turn_bank(nc, psum, identity, [words[:, 2 * b + r, :] for r in range(2)],
-                          0, vw_mx[k], b)
+                rows = [words[:, first_tile + 2 * b + r, :] for r in range(2)]
+                turn_bank(nc, psum, identity, rows, 0, vw_mx[k], b)
 
         def mix_positions(q):
             h = q // 2
@@ -176,7 +177,7 @@ def tile_soablock_pb_kernel(tc, attn, h_x, v_w, v_b, x, out):
                 positions = slice(h * HALF, (h + 1) * HALF)
                 y_in_order = y_bank[:].rearrange("p (j n) -> p n j", j=4)
                 result = out_sb[2 * k + pair][:, r, positions]
-                residual = x_sb[k][:, i, positions]
+                residual = x_sb[k // 2][:, (k % 2) * QUAD + i, positions]
                 tile_bias = bias[:, k * QUAD + i : k * QUAD + i + 1]
                 if r == 0 and h == 0:
                     nc.scalar.activation(

@@ -74,14 +74,16 @@ def tile_soablock_pb_kernel(tc, attn, h_x, v_w, v_b, x, out):
         vw_rows = v_w.rearrange("(p i) c -> p i c", i=QUAD * QUADS)
 
         hx_raw = [keep.tile([P, 2, POS], BF16, name="hx_raw%d" % u) for u in range(2)]
-        at_raw = [keep.tile([P, 4, POS], BF16, name="at_raw%d" % h) for h in range(2)]
+        at_raw = [keep.tile([P, 2, POS], BF16, name="at_raw%d" % q) for q in range(4)]
         vw_raw = [keep.tile([P, 2 * QUAD, MID], BF16, name="vw_raw%d" % d) for d in range(2)]
         x_sb = [keep.tile([P, 2 * QUAD, POS], BF16, name="x_sb%d" % d) for d in range(2)]
 
-        def load_attention(h):
-            half_rows = attn[0, h * HALF : (h + 1) * HALF, :]
+        def load_attention(q):
+            half_rows = attn[0, (q // 2) * HALF : (q // 2 + 1) * HALF, :]
+            first_j = 2 * (q % 2)
             nc.sync.dma_start(
-                out=at_raw[h][:], in_=half_rows.rearrange("(p j) m -> p j m", j=4)
+                out=at_raw[q][:],
+                in_=half_rows.rearrange("(p j) m -> p j m", j=4)[:, first_j : first_j + 2, :],
             )
 
         def load_weights(d):
@@ -97,8 +99,8 @@ def tile_soablock_pb_kernel(tc, attn, h_x, v_w, v_b, x, out):
                 out=hx_raw[u][:],
                 in_=h_x[0].rearrange("(p t) m -> p t m", t=PACK)[:, 2 * u : 2 * (u + 1), :],
             )
-        for h in range(2):
-            load_attention(h)
+        for q in range(4):
+            load_attention(q)
         for d in range(2):
             load_weights(d)
             load_residual(d)
@@ -124,8 +126,8 @@ def tile_soablock_pb_kernel(tc, attn, h_x, v_w, v_b, x, out):
             quantise(nc, hx_mx[u], 0, JOB)
 
         def prepare_attention(q):
-            words = at_raw[q // 2][:].bitcast(F32)
-            rows = [words[:, 2 * (q % 2) + s, :] for s in range(2)]
+            words = at_raw[q][:].bitcast(F32)
+            rows = [words[:, s, :] for s in range(2)]
             for g in range(PASSES_M):
                 turn_bank(nc, psum, identity, rows, g * 2 * P, at_mx[q], g)
             quantise(nc, at_mx[q], 0, JOB)

@@ -25,8 +25,7 @@ QUAD = 4
 QUADS = OUT_CH // (QUAD * P)
 PSUM_BANKS = 8
 STEPS = 4
-TURN_AFTER = 0
-QUANTISE_AFTER = 1
+TURN_EVERY = 3
 
 FLOPS = 2 * MID * POS * POS + 2 * OUT_CH * MID * POS
 
@@ -157,8 +156,7 @@ def tile_soablock_pb_kernel(tc, attn, h_x, v_w, v_b, x, out):
                             start=(g == 0),
                             stop=(g == PASSES_M - 1),
                         )
-                copy = nc.vector.tensor_copy if s == 0 else nc.scalar.copy
-                copy(out=grouped[:, 2 * (q % 2) + s], in_=z_bank[:].rearrange("p t n -> p n t"))
+                nc.scalar.copy(out=grouped[:, 2 * (q % 2) + s], in_=z_bank[:].rearrange("p t n -> p n t"))
             quantise(nc, z_mx[h], (q % 2) * BANK_COLS, BANK_COLS)
 
         out_sb = [keep.tile([P, 2, POS], F32, name="out_sb%d" % r) for r in range(2 * QUADS)]
@@ -212,18 +210,19 @@ def tile_soablock_pb_kernel(tc, attn, h_x, v_w, v_b, x, out):
         prepare_attention(2)
         mix_positions(0)
         prepare_attention(3)
+        mix_positions(1)
         turn_weights(0)
         quantise(nc, vw_mx[0], 0, JOB)
-        mix_positions(1)
         mix_positions(2)
         mix_positions(3)
-        for k in range(QUADS):
-            for step in range(STEPS):
-                pair, h = divmod(step, 2)
-                expand_channels(k, pair, h)
-                if k + 1 < QUADS and step == TURN_AFTER:
-                    turn_weights(k + 1)
-                if k + 1 < QUADS and step == QUANTISE_AFTER:
-                    quantise(nc, vw_mx[k + 1], 0, JOB)
-                if h == 1:
-                    store_pair(k, pair)
+        for step in range(QUADS * STEPS):
+            k, step_of_quad = divmod(step, STEPS)
+            pair, h = divmod(step_of_quad, 2)
+            expand_channels(k, pair, h)
+            turns, late = divmod(step, TURN_EVERY)
+            if turns + 1 < QUADS and late == 0:
+                turn_weights(turns + 1)
+            if turns + 1 < QUADS and late == 1:
+                quantise(nc, vw_mx[turns + 1], 0, JOB)
+            if h == 1:
+                store_pair(k, pair)

from contextlib import ExitStack

import concourse.mybir as mybir
from concourse.masks import make_identity

F32 = mybir.dt.float32
BF16 = mybir.dt.bfloat16
U32 = mybir.dt.uint32
U8 = mybir.dt.uint8
FP8X4 = mybir.dt.float8_e4m3fn_x4
ADD = mybir.AluOpType.add
IDENTITY = mybir.ActivationFunctionType.Identity

P = 128
PACK = 4
K_PASS = P * PACK
POS = 1024
MID = 512
OUT_CH = 2048
HALF = POS // 2
PASSES_M = POS // K_PASS
JOB = 512
BANK_COLS = JOB // 2
QUAD = 4
QUADS = OUT_CH // (QUAD * P)
PSUM_BANKS = 8
STEPS = 4
TURN_EVERY = 3

FLOPS = 2 * MID * POS * POS + 2 * OUT_CH * MID * POS


def mx_tiles(pool, name):
    return {
        "grouped": pool.tile([P, JOB * PACK], BF16, name=name + "_grouped", align_bytes=64),
        "codes": pool.tile([P, JOB], U32, name=name + "_codes", align_bytes=64),
        "scales": pool.tile([P, JOB], U8, name=name + "_scales", align_bytes=64),
    }


def quantise(nc, operand, first_col, cols):
    nc.vector.quantize_mx(
        out=operand["codes"][:, first_col : first_col + cols].bitcast(FP8X4),
        scales=operand["scales"][:, first_col : first_col + cols],
        in_=operand["grouped"][:, first_col * PACK : (first_col + cols) * PACK],
    )


def turn_bank(nc, psum, identity, row_tiles, first_word, operand, bank_index):
    turned = psum.tile([P, 2, BANK_COLS], F32, tag="bank")
    for u in range(2):
        for r in range(2):
            nc.tensor.transpose(
                turned[:, u, r * P : (r + 1) * P],
                row_tiles[r][:, first_word + u : first_word + 2 * P : 2],
                identity[:],
            )
    grouped_words = operand["grouped"][:].bitcast(F32).rearrange(
        "p (b c u) -> p b c u", b=2, u=2
    )
    nc.scalar.copy(out=grouped_words[:, bank_index], in_=turned[:].rearrange("p u c -> p c u"))


def tile_soablock_pb_kernel(tc, attn, h_x, v_w, v_b, x, out):
    nc = tc.nc
    with ExitStack() as ctx:
        ctx.enter_context(tc.manual_schedule())
        keep = ctx.enter_context(tc.tile_pool(name="keep", bufs=1))
        psum = ctx.enter_context(tc.psum_pool(name="psum", bufs=PSUM_BANKS))

        x_rows = x[0].rearrange("(p i) hh ww -> p i (hh ww)", i=QUAD * QUADS)
        out_rows = out[0].rearrange("(p i) hh ww -> p i (hh ww)", i=QUAD * QUADS)
        vw_rows = v_w.rearrange("(p i) c -> p i c", i=QUAD * QUADS)

        hx_raw = [keep.tile([P, 2, POS], BF16, name="hx_raw%d" % u) for u in range(2)]
        at_raw = [keep.tile([P, 2, POS], BF16, name="at_raw%d" % q) for q in range(4)]
        vw_raw = [keep.tile([P, 2 * QUAD, MID], BF16, name="vw_raw%d" % d) for d in range(2)]
        x_sb = [keep.tile([P, 2 * QUAD, POS], BF16, name="x_sb%d" % d) for d in range(2)]

        def load_attention(q):
            half_rows = attn[0, (q // 2) * HALF : (q // 2 + 1) * HALF, :]
            first_j = 2 * (q % 2)
            nc.sync.dma_start(
                out=at_raw[q][:],
                in_=half_rows.rearrange("(p j) m -> p j m", j=4)[:, first_j : first_j + 2, :],
            )

        def load_weights(d):
            rows = slice(d * 2 * QUAD, (d + 1) * 2 * QUAD)
            nc.sync.dma_start(out=vw_raw[d][:], in_=vw_rows[:, rows, :])

        def load_residual(d):
            rows = slice(d * 2 * QUAD, (d + 1) * 2 * QUAD)
            nc.sync.dma_start(out=x_sb[d][:], in_=x_rows[:, rows, :])

        for u in range(2):
            nc.sync.dma_start(
                out=hx_raw[u][:],
                in_=h_x[0].rearrange("(p t) m -> p t m", t=PACK)[:, 2 * u : 2 * (u + 1), :],
            )
        for q in range(4):
            load_attention(q)
        for d in range(2):
            load_weights(d)
            load_residual(d)

        bias_bf16 = keep.tile([P, QUAD * QUADS], BF16)
        nc.scalar.dma_start(out=bias_bf16[:], in_=v_b.rearrange("(p i) -> p i", i=QUAD * QUADS))
        bias = keep.tile([P, QUAD * QUADS], F32)
        nc.scalar.activation(out=bias[:], in_=bias_bf16[:], func=IDENTITY)

        identity = keep.tile([P, P], F32)
        make_identity(nc, identity[:])

        hx_mx = [mx_tiles(keep, "hx%d" % u) for u in range(2)]
        at_mx = [mx_tiles(keep, "at%d" % q) for q in range(4)]
        vw_mx = [mx_tiles(keep, "vw%d" % k) for k in range(QUADS)]
        z_mx = [mx_tiles(keep, "z%d" % h) for h in range(2)]

        def prepare_values(u):
            words = hx_raw[u][:].bitcast(F32)
            for g in range(PASSES_M):
                turn_bank(nc, psum, identity, [words[:, e, :] for e in range(2)],
                          g * 2 * P, hx_mx[u], g)
            quantise(nc, hx_mx[u], 0, JOB)

        def prepare_attention(q):
            words = at_raw[q][:].bitcast(F32)
            rows = [words[:, s, :] for s in range(2)]
            for g in range(PASSES_M):
                turn_bank(nc, psum, identity, rows, g * 2 * P, at_mx[q], g)
            quantise(nc, at_mx[q], 0, JOB)

        def turn_weights(k):
            words = vw_raw[k // 2][:].bitcast(F32)
            first_tile = (k % 2) * QUAD
            for b in range(2):
                rows = [words[:, first_tile + 2 * b + r, :] for r in range(2)]
                turn_bank(nc, psum, identity, rows, 0, vw_mx[k], b)

        def mix_positions(q):
            h = q // 2
            grouped = z_mx[h]["grouped"][:].rearrange("p (j n t) -> p j n t", j=4, t=PACK)
            for s in range(2):
                z_bank = psum.tile([P, PACK, P], F32, tag="bank")
                for t in range(PACK):
                    for g in range(PASSES_M):
                        lhs_cols = slice(g * 2 * P + (t % 2) * P, g * 2 * P + (t % 2 + 1) * P)
                        rhs_cols = slice(g * 2 * P + s * P, g * 2 * P + (s + 1) * P)
                        nc.tensor.matmul_mx(
                            out=z_bank[:, t, :],
                            lhsT=hx_mx[t // 2]["codes"][:, lhs_cols].bitcast(FP8X4),
                            lhsT_scale=hx_mx[t // 2]["scales"][:, lhs_cols],
                            rhs=at_mx[q]["codes"][:, rhs_cols].bitcast(FP8X4),
                            rhs_scale=at_mx[q]["scales"][:, rhs_cols],
                            start=(g == 0),
                            stop=(g == PASSES_M - 1),
                        )
                nc.scalar.copy(out=grouped[:, 2 * (q % 2) + s], in_=z_bank[:].rearrange("p t n -> p n t"))
            quantise(nc, z_mx[h], (q % 2) * BANK_COLS, BANK_COLS)

        out_sb = [keep.tile([P, 2, POS], F32, name="out_sb%d" % r) for r in range(2 * QUADS)]

        def expand_channels(k, pair, h):
            for r in range(2):
                i = 2 * pair + r
                y_bank = psum.tile([P, HALF], F32, tag="bank")
                nc.tensor.matmul_mx(
                    out=y_bank[:],
                    lhsT=vw_mx[k]["codes"][:, i * P : (i + 1) * P].bitcast(FP8X4),
                    lhsT_scale=vw_mx[k]["scales"][:, i * P : (i + 1) * P],
                    rhs=z_mx[h]["codes"][:].bitcast(FP8X4),
                    rhs_scale=z_mx[h]["scales"][:],
                    start=True,
                    stop=True,
                )
                positions = slice(h * HALF, (h + 1) * HALF)
                y_in_order = y_bank[:].rearrange("p (j n) -> p n j", j=4)
                result = out_sb[2 * k + pair][:, r, positions]
                residual = x_sb[k // 2][:, (k % 2) * QUAD + i, positions]
                tile_bias = bias[:, k * QUAD + i : k * QUAD + i + 1]
                if r == 0 and h == 0:
                    nc.scalar.activation(
                        out=result.rearrange("p (n j) -> p n j", j=4),
                        in_=y_in_order,
                        func=IDENTITY,
                        bias=tile_bias,
                    )
                    nc.gpsimd.tensor_tensor(out=result, in0=result, in1=residual, op=ADD)
                else:
                    nc.vector.scalar_tensor_tensor(
                        out=result.rearrange("p (n j) -> p n j", j=4),
                        in0=y_in_order,
                        scalar=tile_bias,
                        in1=residual.rearrange("p (n j) -> p n j", j=4),
                        op0=ADD,
                        op1=ADD,
                    )

        def store_pair(k, pair):
            first_row = k * QUAD + 2 * pair
            nc.sync.dma_start(
                out=out_rows[:, first_row : first_row + 2, :], in_=out_sb[2 * k + pair][:]
            )

        prepare_values(0)
        prepare_values(1)
        prepare_attention(0)
        prepare_attention(1)
        prepare_attention(2)
        mix_positions(0)
        prepare_attention(3)
        mix_positions(1)
        turn_weights(0)
        quantise(nc, vw_mx[0], 0, JOB)
        mix_positions(2)
        mix_positions(3)
        for step in range(QUADS * STEPS):
            k, step_of_quad = divmod(step, STEPS)
            pair, h = divmod(step_of_quad, 2)
            expand_channels(k, pair, h)
            turns, late = divmod(step, TURN_EVERY)
            if turns + 1 < QUADS and late == 0:
                turn_weights(turns + 1)
            if turns + 1 < QUADS and late == 1:
                quantise(nc, vw_mx[turns + 1], 0, JOB)
            if h == 1:
                store_pair(k, pair)
